import numpy as np
import ml_dtypes


def mxq(x, axis, fmt="e4m3"):
    dtype, down = {"e4m3": (ml_dtypes.float8_e4m3fn, 7), "e5m2": (ml_dtypes.float8_e5m2, 14)}[fmt]
    v = np.moveaxis(np.asarray(x, np.float32).astype(ml_dtypes.bfloat16).astype(np.float64), axis, -1)
    blocks = v.reshape(v.shape[:-1] + (-1, 32))
    amax = np.abs(blocks).max(-1, keepdims=True)
    byte = np.maximum(np.where(amax > 0, np.frexp(amax)[1] - 1 + 127, 0) - down, 1)
    scale = np.exp2(byte - 127.0)
    codes = (blocks / scale).astype(np.float32).astype(dtype).astype(np.float64)
    return np.moveaxis((codes * scale).reshape(v.shape), -1, axis)


WIDE = False


def mx_kscale(k):
    if not WIDE:
        return np.ones(k)
    levels = np.array([10, -10, 5, -5, 0])
    a = np.random.permutation(np.resize(levels, k // 512 * 4)).reshape(k // 512, 4)
    idx = np.arange(k)
    return np.exp2(a[idx // 512, idx % 128 // 32])


BF16 = ml_dtypes.bfloat16


def bf(x):
    return np.asarray(x, np.float32).astype(BF16)


def f64(x):
    return np.asarray(x).astype(np.float64)


E2M1 = np.array([0.0, 0.5, 1.0, 1.5, 2.0, 3.0, 4.0, 6.0, -0.0, -0.5, -1.0, -1.5, -2.0, -3.0, -4.0, -6.0])


def pack_weight(w, fmt):
    k, n = w.shape
    w = f64(bf(w)).reshape(k // 32, 32, n)
    amax = np.abs(w).max(1)
    if fmt == "e4m3":
        byte = np.frexp(amax)[1] - 1 + 127 - 7
    else:
        mant, ex = np.frexp(amax / 6.0)
        byte = np.where(mant > 0.5, ex, ex - 1) + 127
    byte = np.clip(np.where(amax > 0, byte, 1), 1, 254)
    scaled = (w * np.exp2(127.0 - byte)[:, None, :]).reshape(k, n).astype(np.float32)
    by_word = np.ascontiguousarray(scaled.reshape(k // 512, 128, 4, n).transpose(0, 1, 3, 2))
    if fmt == "e4m3":
        words = by_word.astype(ml_dtypes.float8_e4m3fn).view(np.uint8)
    else:
        c = by_word.astype(ml_dtypes.float4_e2m1fn).view(np.uint8) & 0xF
        words = c[..., 0::2] | (c[..., 1::2] << 4)
    return np.ascontiguousarray(words), np.ascontiguousarray(byte.astype(np.uint8).reshape(k // 512, 16, n))


def unpack_weight(words, scales, fmt):
    g, p, n, _ = words.shape
    if fmt == "e4m3":
        vals = np.ascontiguousarray(words).view(ml_dtypes.float8_e4m3fn).astype(np.float64)
    else:
        nib = np.empty((g, p, n, 4), np.uint8)
        nib[..., 0::2] = words & 0xF
        nib[..., 1::2] = words >> 4
        vals = E2M1[nib]
    vals = vals * np.repeat(np.exp2(scales.astype(np.float64) - 127.0), 8, axis=1)[..., None]
    return vals.transpose(0, 1, 3, 2).reshape(g * 512, n)


L, R, T, H, F = 4, 4, 256, 1024, 1024


def setup_inputs():
    s, t = mx_kscale(H), mx_kscale(F)
    x = bf(np.random.standard_normal((R, T, H)) * s)
    w_first = np.random.standard_normal((R, H, F)) / np.sqrt(R * H) / s[:, None] * t
    w_second = np.random.standard_normal((R, F, H)) / np.sqrt(R * F) / t[:, None]
    w_first_words, w_first_scales = pack_weight(w_first.reshape(-1, F), "e4m3")
    w_second_words, w_second_scales = pack_weight(w_second.reshape(-1, H), "e4m3")
    return {"x": x,
            "w_first_words": w_first_words, "w_first_scales": w_first_scales,
            "w_second_words": w_second_words, "w_second_scales": w_second_scales}


def reference(x, w_first_words, w_first_scales, w_second_words, w_second_scales):
    y = mxq(f64(x), 2, "e4m3") @ unpack_weight(w_first_words, w_first_scales, "e4m3").reshape(R, H, F)
    reduced = y.sum(0)
    z = mxq(reduced, 1, "e4m3")[None] @ unpack_weight(w_second_words, w_second_scales, "e4m3").reshape(R, F, H)
    total = z.sum(0)
    return np.broadcast_to(total[None], z.shape).copy()

@@ -1,0 +1,170 @@
+from contextlib import ExitStack
+
+import concourse.mybir as mybir
+from concourse.masks import make_identity
+
+F32 = mybir.dt.float32
+BF16 = mybir.dt.bfloat16
+I32 = mybir.dt.int32
+U8 = mybir.dt.uint8
+FP8X4 = mybir.dt.float8_e4m3fn_x4
+
+P = 128
+PACK = 4
+K_PASS = P * PACK
+RANKS = 4
+TOKENS = 256
+WIDTH = 1024
+TOKEN_TILES = TOKENS // P
+N_TILE = 512
+COL_TILES = WIDTH // N_TILE
+PASSES = RANKS * WIDTH // K_PASS
+PASSES_PER_RANK = WIDTH // K_PASS
+PLANES_PER_TILE = 4
+PLANE_BLOCKS = PASSES // PLANES_PER_TILE
+
+FLOPS = 2 * 2 * TOKENS * RANKS * WIDTH * WIDTH
+
+
+def load_weight(nc, words_dram, words):
+    for g in range(PASSES):
+        nc.sync.dma_start(
+            out=words[:, g, :],
+            in_=words_dram[g].rearrange("p n t -> p (n t)").bitcast(I32),
+        )
+
+
+def load_scale_planes(nc, scales_dram, planes):
+    for b in range(PLANE_BLOCKS):
+        for quadrant in range(4):
+            nc.sync.dma_start(
+                out=planes[32 * quadrant : 32 * quadrant + 16, b, :].bitcast(I32),
+                in_=scales_dram[
+                    PLANES_PER_TILE * b : PLANES_PER_TILE * (b + 1), 4 * quadrant : 4 * quadrant + 4, :
+                ].bitcast(I32),
+            )
+
+
+def weight_pass(nc, acc, codes, code_scales, words, planes, g, c):
+    cols = slice(c * N_TILE, (c + 1) * N_TILE)
+    nc.tensor.matmul_mx(
+        out=acc[:],
+        lhsT=codes.bitcast(FP8X4),
+        lhsT_scale=code_scales,
+        rhs=words[:, g, cols].bitcast(FP8X4),
+        rhs_scale=planes[4 * (g % PLANES_PER_TILE) : P, g // PLANES_PER_TILE, cols],
+        start=(g == 0),
+        stop=(g == PASSES - 1),
+    )
+
+
+def copy_on(nc, index, out, in_):
+    if index % 2 == 0:
+        nc.scalar.copy(out=out, in_=in_)
+    else:
+        nc.vector.tensor_copy(out=out, in_=in_)
+
+
+def tile_multilayerallreduce_pa_e_kernel(
+    tc, x, w_first_words, w_first_scales, w_second_words, w_second_scales, out
+):
+    nc = tc.nc
+    with ExitStack() as stack:
+        keep = stack.enter_context(tc.tile_pool(name="keep", bufs=1))
+        stage = stack.enter_context(tc.tile_pool(name="stage", bufs=4))
+        psum_t = stack.enter_context(tc.psum_pool(name="psum_t", bufs=4))
+        psum_acc = stack.enter_context(tc.psum_pool(name="psum_acc", bufs=4))
+
+        w1_planes = keep.tile([P, PLANE_BLOCKS, WIDTH], U8, align_bytes=64)
+        w2_planes = keep.tile([P, PLANE_BLOCKS, WIDTH], U8, align_bytes=64)
+        nc.vector.memset(w1_planes[:].bitcast(I32), 0)
+        nc.vector.memset(w2_planes[:].bitcast(I32), 0)
+
+        ident_f32 = keep.tile([P, P], F32)
+        make_identity(nc, ident_f32[:])
+        ident_bf16 = keep.tile([P, P], BF16)
+        make_identity(nc, ident_bf16[:])
+
+        x_sb = keep.tile([P, RANKS, TOKEN_TILES, WIDTH], BF16)
+        for r in range(RANKS):
+            nc.sync.dma_start(out=x_sb[:, r], in_=x[r].rearrange("(p h) k -> p h k", h=TOKEN_TILES))
+        load_scale_planes(nc, w_first_scales, w1_planes)
+        load_scale_planes(nc, w_second_scales, w2_planes)
+        w1_words = keep.tile([P, PASSES, WIDTH], I32, align_bytes=64)
+        w2_words = keep.tile([P, PASSES, WIDTH], I32, align_bytes=64)
+        load_weight(nc, w_first_words, w1_words)
+        load_weight(nc, w_second_words, w2_words)
+
+        x_codes = keep.tile([P, PASSES, TOKENS], I32, align_bytes=64)
+        x_scales = keep.tile([P, PASSES, TOKENS], U8, align_bytes=64)
+        for g in range(PASSES):
+            r, kh = divmod(g, PASSES_PER_RANK)
+            xt = psum_t.tile([P, TOKEN_TILES, 2, P], F32, tag="transposed")
+            for h in range(TOKEN_TILES):
+                words_of_x = x_sb[:, r, h, :].bitcast(F32)
+                for u in range(2):
+                    nc.tensor.transpose(
+                        xt[:, h, u, :],
+                        words_of_x[:, 256 * kh + u : 256 * (kh + 1) : 2],
+                        ident_f32[:],
+                    )
+            x_grouped = stage.tile([P, TOKENS * PACK], BF16, align_bytes=64)
+            copy_on(
+                nc,
+                g,
+                out=x_grouped[:].bitcast(F32).rearrange("p (h i u) -> p h i u", h=TOKEN_TILES, u=2),
+                in_=xt[:].rearrange("p h u i -> p h i u"),
+            )
+            nc.vector.quantize_mx(
+                out=x_codes[:, g, :].bitcast(FP8X4), scales=x_scales[:, g, :], in_=x_grouped[:]
+            )
+
+        reduced = [
+            [psum_acc.tile([P, N_TILE], F32, name="reduced_%d_%d" % (h, c), tag="acc") for c in range(COL_TILES)]
+            for h in range(TOKEN_TILES)
+        ]
+        for g in range(PASSES):
+            for h in range(TOKEN_TILES):
+                tokens = slice(h * P, (h + 1) * P)
+                for c in range(COL_TILES):
+                    weight_pass(
+                        nc, reduced[h][c], x_codes[:, g, tokens], x_scales[:, g, tokens], w1_words, w1_planes, g, c
+                    )
+
+        red_codes = keep.tile([P, TOKEN_TILES, COL_TILES, P], I32, align_bytes=64)
+        red_scales = keep.tile([P, TOKEN_TILES, COL_TILES, P], U8, align_bytes=64)
+        red_bf16 = keep.tile([P, TOKEN_TILES, COL_TILES, PACK, P], BF16)
+        red_grouped = keep.tile([P, TOKEN_TILES, COL_TILES * P * PACK], BF16, align_bytes=64)
+        for h in range(TOKEN_TILES):
+            for c in range(COL_TILES):
+                copy_on(nc, c, out=red_bf16[:, h, c], in_=reduced[h][c][:].rearrange("p (q t) -> p t q", t=PACK))
+        for h in range(TOKEN_TILES):
+            for c in range(COL_TILES):
+                rt = psum_t.tile([P, PACK, P], BF16, tag="transposed")
+                for t in range(PACK):
+                    nc.tensor.transpose(rt[:, t, :], red_bf16[:, h, c, t, :], ident_bf16[:])
+                copy_on(
+                    nc,
+                    c,
+                    out=red_grouped[:, h, c * P * PACK : (c + 1) * P * PACK].rearrange("p (i t) -> p i t", t=PACK),
+                    in_=rt[:].rearrange("p t i -> p i t"),
+                )
+            nc.vector.quantize_mx(
+                out=red_codes[:, h].rearrange("p c i -> p (c i)").bitcast(FP8X4),
+                scales=red_scales[:, h].rearrange("p c i -> p (c i)"),
+                in_=red_grouped[:, h, :],
+            )
+
+        result = keep.tile([P, TOKEN_TILES, WIDTH], F32)
+        for h in range(TOKEN_TILES):
+            total = [psum_acc.tile([P, N_TILE], F32, name="total_%d_%d" % (h, c), tag="acc") for c in range(COL_TILES)]
+            for g in range(PASSES):
+                kh = g % PASSES_PER_RANK
+                for c in range(COL_TILES):
+                    weight_pass(nc, total[c], red_codes[:, h, kh, :], red_scales[:, h, kh, :], w2_words, w2_planes, g, c)
+            for c in range(COL_TILES):
+                copy_on(nc, c, out=result[:, h, c * N_TILE : (c + 1) * N_TILE], in_=total[c][:])
+            for r in range(RANKS):
+                nc.sync.dma_start(
+                    out=out[r].rearrange("(p h) n -> p h n", h=TOKEN_TILES)[:, h, :], in_=result[:, h, :]
+                )

@@ -26,11 +26,11 @@ PLANE_BLOCKS = PASSES // PLANES_PER_TILE
 FLOPS = 2 * 2 * TOKENS * RANKS * WIDTH * WIDTH
 
 
-def load_weight(nc, words_dram, words):
+def load_weight(nc, words_dram, words, cols):
     for g in range(PASSES):
         nc.sync.dma_start(
-            out=words[:, g, :],
-            in_=words_dram[g].rearrange("p n t -> p (n t)").bitcast(I32),
+            out=words[:, g, cols],
+            in_=words_dram[g, :, cols, :].rearrange("p n t -> p (n t)").bitcast(I32),
         )
 
 
@@ -74,6 +74,7 @@ def tile_multilayerallreduce_pa_e_kernel(
         stage = stack.enter_context(tc.tile_pool(name="stage", bufs=4))
         psum_t = stack.enter_context(tc.psum_pool(name="psum_t", bufs=4))
         psum_acc = stack.enter_context(tc.psum_pool(name="psum_acc", bufs=4))
+        stack.enter_context(tc.manual_schedule())
 
         w1_planes = keep.tile([P, PLANE_BLOCKS, WIDTH], U8, align_bytes=64)
         w2_planes = keep.tile([P, PLANE_BLOCKS, WIDTH], U8, align_bytes=64)
@@ -92,11 +93,19 @@ def tile_multilayerallreduce_pa_e_kernel(
         load_scale_planes(nc, w_second_scales, w2_planes)
         w1_words = keep.tile([P, PASSES, WIDTH], I32, align_bytes=64)
         w2_words = keep.tile([P, PASSES, WIDTH], I32, align_bytes=64)
-        load_weight(nc, w_first_words, w1_words)
-        load_weight(nc, w_second_words, w2_words)
+        load_weight(nc, w_first_words, w1_words, slice(0, WIDTH))
+        for c in range(COL_TILES):
+            load_weight(nc, w_second_words, w2_words, slice(c * N_TILE, (c + 1) * N_TILE))
 
         x_codes = keep.tile([P, PASSES, TOKENS], I32, align_bytes=64)
         x_scales = keep.tile([P, PASSES, TOKENS], U8, align_bytes=64)
+        x_grouped = [None] * PASSES
+
+        def quantise_x(g):
+            nc.vector.quantize_mx(
+                out=x_codes[:, g, :].bitcast(FP8X4), scales=x_scales[:, g, :], in_=x_grouped[g][:]
+            )
+
         for g in range(PASSES):
             r, kh = divmod(g, PASSES_PER_RANK)
             xt = psum_t.tile([P, TOKEN_TILES, 2, P], F32, tag="transposed")
@@ -108,16 +117,16 @@ def tile_multilayerallreduce_pa_e_kernel(
                         words_of_x[:, 256 * kh + u : 256 * (kh + 1) : 2],
                         ident_f32[:],
                     )
-            x_grouped = stage.tile([P, TOKENS * PACK], BF16, align_bytes=64)
+            x_grouped[g] = stage.tile([P, TOKENS * PACK], BF16, name="x_grouped", align_bytes=64)
             copy_on(
                 nc,
                 g,
-                out=x_grouped[:].bitcast(F32).rearrange("p (h i u) -> p h i u", h=TOKEN_TILES, u=2),
+                out=x_grouped[g][:].bitcast(F32).rearrange("p (h i u) -> p h i u", h=TOKEN_TILES, u=2),
                 in_=xt[:].rearrange("p h u i -> p h i u"),
             )
-            nc.vector.quantize_mx(
-                out=x_codes[:, g, :].bitcast(FP8X4), scales=x_scales[:, g, :], in_=x_grouped[:]
-            )
+            if g > 0:
+                quantise_x(g - 1)
+        quantise_x(PASSES - 1)
 
         reduced = [
             [psum_acc.tile([P, N_TILE], F32, name="reduced_%d_%d" % (h, c), tag="acc") for c in range(COL_TILES)]
@@ -156,15 +165,15 @@ def tile_multilayerallreduce_pa_e_kernel(
             )
 
         result = keep.tile([P, TOKEN_TILES, WIDTH], F32)
-        for h in range(TOKEN_TILES):
-            total = [psum_acc.tile([P, N_TILE], F32, name="total_%d_%d" % (h, c), tag="acc") for c in range(COL_TILES)]
-            for g in range(PASSES):
-                kh = g % PASSES_PER_RANK
-                for c in range(COL_TILES):
-                    weight_pass(nc, total[c], red_codes[:, h, kh, :], red_scales[:, h, kh, :], w2_words, w2_planes, g, c)
-            for c in range(COL_TILES):
-                copy_on(nc, c, out=result[:, h, c * N_TILE : (c + 1) * N_TILE], in_=total[c][:])
-            for r in range(RANKS):
-                nc.sync.dma_start(
-                    out=out[r].rearrange("(p h) n -> p h n", h=TOKEN_TILES)[:, h, :], in_=result[:, h, :]
-                )
+        for c in range(COL_TILES):
+            cols = slice(c * N_TILE, (c + 1) * N_TILE)
+            for h in range(TOKEN_TILES):
+                total = psum_acc.tile([P, N_TILE], F32, tag="acc")
+                for g in range(PASSES):
+                    kh = g % PASSES_PER_RANK
+                    weight_pass(nc, total, red_codes[:, h, kh, :], red_scales[:, h, kh, :], w2_words, w2_planes, g, c)
+                copy_on(nc, h, out=result[:, h, cols], in_=total[:])
+                for r in range(RANKS):
+                    nc.sync.dma_start(
+                        out=out[r].rearrange("(p h) n -> p h n", h=TOKEN_TILES)[:, h, cols], in_=result[:, h, cols]
+                    )

@@ -26,23 +26,22 @@ PLANE_BLOCKS = PASSES // PLANES_PER_TILE
 FLOPS = 2 * 2 * TOKENS * RANKS * WIDTH * WIDTH
 
 
-def load_weight(nc, words_dram, words, cols):
-    for g in range(PASSES):
+def load_words(nc, words_dram, words, passes, cols):
+    for g in passes:
         nc.sync.dma_start(
             out=words[:, g, cols],
             in_=words_dram[g, :, cols, :].rearrange("p n t -> p (n t)").bitcast(I32),
         )
 
 
-def load_scale_planes(nc, scales_dram, planes):
-    for b in range(PLANE_BLOCKS):
-        for quadrant in range(4):
-            nc.sync.dma_start(
-                out=planes[32 * quadrant : 32 * quadrant + 16, b, :].bitcast(I32),
-                in_=scales_dram[
-                    PLANES_PER_TILE * b : PLANES_PER_TILE * (b + 1), 4 * quadrant : 4 * quadrant + 4, :
-                ].bitcast(I32),
-            )
+def load_scale_planes(nc, scales_dram, planes, b):
+    for quadrant in range(4):
+        nc.sync.dma_start(
+            out=planes[32 * quadrant : 32 * quadrant + 16, b, :].bitcast(I32),
+            in_=scales_dram[
+                PLANES_PER_TILE * b : PLANES_PER_TILE * (b + 1), 4 * quadrant : 4 * quadrant + 4, :
+            ].bitcast(I32),
+        )
 
 
 def weight_pass(nc, acc, codes, code_scales, words, planes, g, c):
@@ -87,15 +86,19 @@ def tile_multilayerallreduce_pa_e_kernel(
         make_identity(nc, ident_bf16[:])
 
         x_sb = keep.tile([P, RANKS, TOKEN_TILES, WIDTH], BF16)
-        for r in range(RANKS):
-            nc.sync.dma_start(out=x_sb[:, r], in_=x[r].rearrange("(p h) k -> p h k", h=TOKEN_TILES))
-        load_scale_planes(nc, w_first_scales, w1_planes)
-        load_scale_planes(nc, w_second_scales, w2_planes)
         w1_words = keep.tile([P, PASSES, WIDTH], I32, align_bytes=64)
         w2_words = keep.tile([P, PASSES, WIDTH], I32, align_bytes=64)
-        load_weight(nc, w_first_words, w1_words, slice(0, WIDTH))
+        all_cols = slice(0, WIDTH)
+        load_scale_planes(nc, w_first_scales, w1_planes, 0)
+        for r in range(RANKS):
+            nc.sync.dma_start(out=x_sb[:, r], in_=x[r].rearrange("(p h) k -> p h k", h=TOKEN_TILES))
+        load_scale_planes(nc, w_first_scales, w1_planes, 1)
+        load_words(nc, w_first_words, w1_words, range(0, 4), all_cols)
+        load_scale_planes(nc, w_second_scales, w2_planes, 0)
+        load_words(nc, w_first_words, w1_words, range(4, PASSES), all_cols)
+        load_scale_planes(nc, w_second_scales, w2_planes, 1)
         for c in range(COL_TILES):
-            load_weight(nc, w_second_words, w2_words, slice(c * N_TILE, (c + 1) * N_TILE))
+            load_words(nc, w_second_words, w2_words, range(PASSES), slice(c * N_TILE, (c + 1) * N_TILE))
 
         x_codes = keep.tile([P, PASSES, TOKENS], I32, align_bytes=64)
         x_scales = keep.tile([P, PASSES, TOKENS], U8, align_bytes=64)

@@ -89,9 +89,14 @@ def tile_multilayerallreduce_pa_e_kernel(
         w1_words = keep.tile([P, PASSES, WIDTH], I32, align_bytes=64)
         w2_words = keep.tile([P, PASSES, WIDTH], I32, align_bytes=64)
         all_cols = slice(0, WIDTH)
+
+        def load_x(ranks):
+            for r in ranks:
+                nc.sync.dma_start(out=x_sb[:, r], in_=x[r].rearrange("(p h) k -> p h k", h=TOKEN_TILES))
+
+        load_x(range(0, 2))
         load_scale_planes(nc, w_first_scales, w1_planes, 0)
-        for r in range(RANKS):
-            nc.sync.dma_start(out=x_sb[:, r], in_=x[r].rearrange("(p h) k -> p h k", h=TOKEN_TILES))
+        load_x(range(2, RANKS))
         load_scale_planes(nc, w_first_scales, w1_planes, 1)
         load_words(nc, w_first_words, w1_words, range(0, 4), all_cols)
         load_scale_planes(nc, w_second_scales, w2_planes, 0)

@@ -181,7 +181,7 @@ def tile_multilayerallreduce_pa_e_kernel(
                     kh = g % PASSES_PER_RANK
                     weight_pass(nc, total, red_codes[:, h, kh, :], red_scales[:, h, kh, :], w2_words, w2_planes, g, c)
                 copy_on(nc, h, out=result[:, h, cols], in_=total[:])
-                for r in range(RANKS):
-                    nc.sync.dma_start(
-                        out=out[r].rearrange("(p h) n -> p h n", h=TOKEN_TILES)[:, h, cols], in_=result[:, h, cols]
-                    )
+                nc.sync.dma_start(
+                    out=out.rearrange("r (p h) n -> p r h n", h=TOKEN_TILES)[:, :, h, cols],
+                    in_=result[:, h, cols].unsqueeze(1).to_broadcast([P, RANKS, N_TILE]),
+                )

@@ -97,13 +97,14 @@ def tile_multilayerallreduce_pa_e_kernel(
         load_x(range(0, 2))
         load_scale_planes(nc, w_first_scales, w1_planes, 0)
         load_x(range(2, RANKS))
+        load_words(nc, w_first_words, w1_words, range(0, 2), all_cols)
         load_scale_planes(nc, w_first_scales, w1_planes, 1)
-        load_words(nc, w_first_words, w1_words, range(0, 4), all_cols)
+        load_words(nc, w_first_words, w1_words, range(2, PASSES), all_cols)
         load_scale_planes(nc, w_second_scales, w2_planes, 0)
-        load_words(nc, w_first_words, w1_words, range(4, PASSES), all_cols)
+        load_words(nc, w_second_words, w2_words, range(0, 4), slice(0, N_TILE))
         load_scale_planes(nc, w_second_scales, w2_planes, 1)
-        for c in range(COL_TILES):
-            load_words(nc, w_second_words, w2_words, range(PASSES), slice(c * N_TILE, (c + 1) * N_TILE))
+        load_words(nc, w_second_words, w2_words, range(4, PASSES), slice(0, N_TILE))
+        load_words(nc, w_second_words, w2_words, range(PASSES), slice(N_TILE, WIDTH))
 
         x_codes = keep.tile([P, PASSES, TOKENS], I32, align_bytes=64)
         x_scales = keep.tile([P, PASSES, TOKENS], U8, align_bytes=64)

@@ -27,20 +27,18 @@ FLOPS = 2 * 2 * TOKENS * RANKS * WIDTH * WIDTH
 
 
 def load_words(nc, words_dram, words, passes, cols):
-    for g in passes:
+    for slot, g in passes:
         nc.sync.dma_start(
-            out=words[:, g, cols],
+            out=words[:, slot, cols],
             in_=words_dram[g, :, cols, :].rearrange("p n t -> p (n t)").bitcast(I32),
         )
 
 
-def load_scale_planes(nc, scales_dram, planes, b):
+def load_scale_planes(nc, scales_dram, planes, b, four):
     for quadrant in range(4):
         nc.sync.dma_start(
             out=planes[32 * quadrant : 32 * quadrant + 16, b, :].bitcast(I32),
-            in_=scales_dram[
-                PLANES_PER_TILE * b : PLANES_PER_TILE * (b + 1), 4 * quadrant : 4 * quadrant + 4, :
-            ].bitcast(I32),
+            in_=scales_dram[four, 4 * quadrant : 4 * quadrant + 4, :].bitcast(I32),
         )
 
 
@@ -95,16 +93,17 @@ def tile_multilayerallreduce_pa_e_kernel(
                 nc.sync.dma_start(out=x_sb[:, r], in_=x[r].rearrange("(p h) k -> p h k", h=TOKEN_TILES))
 
         load_x(range(0, 2))
-        load_scale_planes(nc, w_first_scales, w1_planes, 0)
+        load_scale_planes(nc, w_first_scales, w1_planes, 0, slice(0, 4))
         load_x(range(2, RANKS))
-        load_words(nc, w_first_words, w1_words, range(0, 2), all_cols)
-        load_scale_planes(nc, w_first_scales, w1_planes, 1)
-        load_words(nc, w_first_words, w1_words, range(2, PASSES), all_cols)
-        load_scale_planes(nc, w_second_scales, w2_planes, 0)
-        load_words(nc, w_second_words, w2_words, range(0, 4), slice(0, N_TILE))
-        load_scale_planes(nc, w_second_scales, w2_planes, 1)
-        load_words(nc, w_second_words, w2_words, range(4, PASSES), slice(0, N_TILE))
-        load_words(nc, w_second_words, w2_words, range(PASSES), slice(N_TILE, WIDTH))
+        load_words(nc, w_first_words, w1_words, [(g, g) for g in range(0, 2)], all_cols)
+        load_scale_planes(nc, w_first_scales, w1_planes, 1, slice(4, 8))
+        load_words(nc, w_first_words, w1_words, [(g, g) for g in range(2, PASSES)], all_cols)
+        load_scale_planes(nc, w_second_scales, w2_planes, 0, slice(0, 8, 2))
+        w2_order = [(RANKS * kh + r, PASSES_PER_RANK * r + kh) for kh in range(PASSES_PER_RANK) for r in range(RANKS)]
+        load_words(nc, w_second_words, w2_words, w2_order[:RANKS], slice(0, N_TILE))
+        load_scale_planes(nc, w_second_scales, w2_planes, 1, slice(1, 8, 2))
+        load_words(nc, w_second_words, w2_words, w2_order[RANKS:], slice(0, N_TILE))
+        load_words(nc, w_second_words, w2_words, w2_order, slice(N_TILE, WIDTH))
 
         x_codes = keep.tile([P, PASSES, TOKENS], I32, align_bytes=64)
         x_scales = keep.tile([P, PASSES, TOKENS], U8, align_bytes=64)
@@ -167,11 +166,12 @@ def tile_multilayerallreduce_pa_e_kernel(
                     out=red_grouped[:, h, c * P * PACK : (c + 1) * P * PACK].rearrange("p (i t) -> p i t", t=PACK),
                     in_=rt[:].rearrange("p t i -> p i t"),
                 )
-            nc.vector.quantize_mx(
-                out=red_codes[:, h].rearrange("p c i -> p (c i)").bitcast(FP8X4),
-                scales=red_scales[:, h].rearrange("p c i -> p (c i)"),
-                in_=red_grouped[:, h, :],
-            )
+            for c in range(COL_TILES):
+                nc.vector.quantize_mx(
+                    out=red_codes[:, h, c, :].bitcast(FP8X4),
+                    scales=red_scales[:, h, c, :],
+                    in_=red_grouped[:, h, c * P * PACK : (c + 1) * P * PACK],
+                )
 
         result = keep.tile([P, TOKEN_TILES, WIDTH], F32)
         for c in range(COL_TILES):
@@ -179,7 +179,7 @@ def tile_multilayerallreduce_pa_e_kernel(
             for h in range(TOKEN_TILES):
                 total = psum_acc.tile([P, N_TILE], F32, tag="acc")
                 for g in range(PASSES):
-                    kh = g % PASSES_PER_RANK
+                    kh = g // RANKS
                     weight_pass(nc, total, red_codes[:, h, kh, :], red_scales[:, h, kh, :], w2_words, w2_planes, g, c)
                 copy_on(nc, h, out=result[:, h, cols], in_=total[:])
                 nc.sync.dma_start(

@@ -34,11 +34,11 @@ def load_words(nc, words_dram, words, passes, cols):
         )
 
 
-def load_scale_planes(nc, scales_dram, planes, b, four):
+def load_scale_planes(queue, view, scales_dram, planes, b, four):
     for quadrant in range(4):
-        nc.sync.dma_start(
-            out=planes[32 * quadrant : 32 * quadrant + 16, b, :].bitcast(I32),
-            in_=scales_dram[four, 4 * quadrant : 4 * quadrant + 4, :].bitcast(I32),
+        queue.dma_start(
+            out=planes[32 * quadrant : 32 * quadrant + 16, b, :].bitcast(view),
+            in_=scales_dram[four, 4 * quadrant : 4 * quadrant + 4, :].bitcast(view),
         )
 
 
@@ -80,6 +80,7 @@ def tile_multilayerallreduce_pa_e_kernel(
 
         ident_f32 = keep.tile([P, P], F32)
         make_identity(nc, ident_f32[:])
+        load_scale_planes(nc.gpsimd, F32, w_first_scales, w1_planes, 1, slice(4, 8))
         ident_bf16 = keep.tile([P, P], BF16)
         make_identity(nc, ident_bf16[:])
 
@@ -93,15 +94,14 @@ def tile_multilayerallreduce_pa_e_kernel(
                 nc.sync.dma_start(out=x_sb[:, r], in_=x[r].rearrange("(p h) k -> p h k", h=TOKEN_TILES))
 
         load_x(range(0, 2))
-        load_scale_planes(nc, w_first_scales, w1_planes, 0, slice(0, 4))
+        load_scale_planes(nc.sync, I32, w_first_scales, w1_planes, 0, slice(0, 4))
         load_x(range(2, RANKS))
         load_words(nc, w_first_words, w1_words, [(g, g) for g in range(0, 2)], all_cols)
-        load_scale_planes(nc, w_first_scales, w1_planes, 1, slice(4, 8))
         load_words(nc, w_first_words, w1_words, [(g, g) for g in range(2, PASSES)], all_cols)
-        load_scale_planes(nc, w_second_scales, w2_planes, 0, slice(0, 8, 2))
+        load_scale_planes(nc.sync, I32, w_second_scales, w2_planes, 0, slice(0, 8, 2))
         w2_order = [(RANKS * kh + r, PASSES_PER_RANK * r + kh) for kh in range(PASSES_PER_RANK) for r in range(RANKS)]
         load_words(nc, w_second_words, w2_words, w2_order[:RANKS], slice(0, N_TILE))
-        load_scale_planes(nc, w_second_scales, w2_planes, 1, slice(1, 8, 2))
+        load_scale_planes(nc.sync, I32, w_second_scales, w2_planes, 1, slice(1, 8, 2))
         load_words(nc, w_second_words, w2_words, w2_order[RANKS:], slice(0, N_TILE))
         load_words(nc, w_second_words, w2_words, w2_order, slice(N_TILE, WIDTH))
 

from contextlib import ExitStack

import concourse.mybir as mybir
from concourse.masks import make_identity

F32 = mybir.dt.float32
BF16 = mybir.dt.bfloat16
I32 = mybir.dt.int32
U8 = mybir.dt.uint8
FP8X4 = mybir.dt.float8_e4m3fn_x4

P = 128
PACK = 4
K_PASS = P * PACK
RANKS = 4
TOKENS = 256
WIDTH = 1024
TOKEN_TILES = TOKENS // P
N_TILE = 512
COL_TILES = WIDTH // N_TILE
PASSES = RANKS * WIDTH // K_PASS
PASSES_PER_RANK = WIDTH // K_PASS
PLANES_PER_TILE = 4
PLANE_BLOCKS = PASSES // PLANES_PER_TILE

FLOPS = 2 * 2 * TOKENS * RANKS * WIDTH * WIDTH


def load_words(nc, words_dram, words, passes, cols):
    for slot, g in passes:
        nc.sync.dma_start(
            out=words[:, slot, cols],
            in_=words_dram[g, :, cols, :].rearrange("p n t -> p (n t)").bitcast(I32),
        )


def load_scale_planes(queue, view, scales_dram, planes, b, four):
    for quadrant in range(4):
        queue.dma_start(
            out=planes[32 * quadrant : 32 * quadrant + 16, b, :].bitcast(view),
            in_=scales_dram[four, 4 * quadrant : 4 * quadrant + 4, :].bitcast(view),
        )


def weight_pass(nc, acc, codes, code_scales, words, planes, g, c):
    cols = slice(c * N_TILE, (c + 1) * N_TILE)
    nc.tensor.matmul_mx(
        out=acc[:],
        lhsT=codes.bitcast(FP8X4),
        lhsT_scale=code_scales,
        rhs=words[:, g, cols].bitcast(FP8X4),
        rhs_scale=planes[4 * (g % PLANES_PER_TILE) : P, g // PLANES_PER_TILE, cols],
        start=(g == 0),
        stop=(g == PASSES - 1),
    )


def copy_on(nc, index, out, in_):
    if index % 2 == 0:
        nc.scalar.copy(out=out, in_=in_)
    else:
        nc.vector.tensor_copy(out=out, in_=in_)


def tile_multilayerallreduce_pa_e_kernel(
    tc, x, w_first_words, w_first_scales, w_second_words, w_second_scales, out
):
    nc = tc.nc
    with ExitStack() as stack:
        keep = stack.enter_context(tc.tile_pool(name="keep", bufs=1))
        stage = stack.enter_context(tc.tile_pool(name="stage", bufs=4))
        psum_t = stack.enter_context(tc.psum_pool(name="psum_t", bufs=4))
        psum_acc = stack.enter_context(tc.psum_pool(name="psum_acc", bufs=4))
        stack.enter_context(tc.manual_schedule())

        w1_planes = keep.tile([P, PLANE_BLOCKS, WIDTH], U8, align_bytes=64)
        w2_planes = keep.tile([P, PLANE_BLOCKS, WIDTH], U8, align_bytes=64)
        nc.vector.memset(w1_planes[:].bitcast(I32), 0)
        nc.vector.memset(w2_planes[:].bitcast(I32), 0)

        ident_f32 = keep.tile([P, P], F32)
        make_identity(nc, ident_f32[:])
        load_scale_planes(nc.gpsimd, F32, w_first_scales, w1_planes, 1, slice(4, 8))
        ident_bf16 = keep.tile([P, P], BF16)
        make_identity(nc, ident_bf16[:])

        x_sb = keep.tile([P, RANKS, TOKEN_TILES, WIDTH], BF16)
        w1_words = keep.tile([P, PASSES, WIDTH], I32, align_bytes=64)
        w2_words = keep.tile([P, PASSES, WIDTH], I32, align_bytes=64)
        all_cols = slice(0, WIDTH)

        def load_x(ranks):
            for r in ranks:
                nc.sync.dma_start(out=x_sb[:, r], in_=x[r].rearrange("(p h) k -> p h k", h=TOKEN_TILES))

        load_x(range(0, 2))
        load_scale_planes(nc.sync, I32, w_first_scales, w1_planes, 0, slice(0, 4))
        load_x(range(2, RANKS))
        load_words(nc, w_first_words, w1_words, [(g, g) for g in range(0, 2)], all_cols)
        load_words(nc, w_first_words, w1_words, [(g, g) for g in range(2, PASSES)], all_cols)
        load_scale_planes(nc.sync, I32, w_second_scales, w2_planes, 0, slice(0, 8, 2))
        w2_order = [(RANKS * kh + r, PASSES_PER_RANK * r + kh) for kh in range(PASSES_PER_RANK) for r in range(RANKS)]
        load_words(nc, w_second_words, w2_words, w2_order[:RANKS], slice(0, N_TILE))
        load_scale_planes(nc.sync, I32, w_second_scales, w2_planes, 1, slice(1, 8, 2))
        load_words(nc, w_second_words, w2_words, w2_order[RANKS:], slice(0, N_TILE))
        load_words(nc, w_second_words, w2_words, w2_order, slice(N_TILE, WIDTH))

        x_codes = keep.tile([P, PASSES, TOKENS], I32, align_bytes=64)
        x_scales = keep.tile([P, PASSES, TOKENS], U8, align_bytes=64)
        x_grouped = [None] * PASSES

        def quantise_x(g):
            nc.vector.quantize_mx(
                out=x_codes[:, g, :].bitcast(FP8X4), scales=x_scales[:, g, :], in_=x_grouped[g][:]
            )

        for g in range(PASSES):
            r, kh = divmod(g, PASSES_PER_RANK)
            xt = psum_t.tile([P, TOKEN_TILES, 2, P], F32, tag="transposed")
            for h in range(TOKEN_TILES):
                words_of_x = x_sb[:, r, h, :].bitcast(F32)
                for u in range(2):
                    nc.tensor.transpose(
                        xt[:, h, u, :],
                        words_of_x[:, 256 * kh + u : 256 * (kh + 1) : 2],
                        ident_f32[:],
                    )
            x_grouped[g] = stage.tile([P, TOKENS * PACK], BF16, name="x_grouped", align_bytes=64)
            copy_on(
                nc,
                g,
                out=x_grouped[g][:].bitcast(F32).rearrange("p (h i u) -> p h i u", h=TOKEN_TILES, u=2),
                in_=xt[:].rearrange("p h u i -> p h i u"),
            )
            if g > 0:
                quantise_x(g - 1)
        quantise_x(PASSES - 1)

        reduced = [
            [psum_acc.tile([P, N_TILE], F32, name="reduced_%d_%d" % (h, c), tag="acc") for c in range(COL_TILES)]
            for h in range(TOKEN_TILES)
        ]
        for g in range(PASSES):
            for h in range(TOKEN_TILES):
                tokens = slice(h * P, (h + 1) * P)
                for c in range(COL_TILES):
                    weight_pass(
                        nc, reduced[h][c], x_codes[:, g, tokens], x_scales[:, g, tokens], w1_words, w1_planes, g, c
                    )

        red_codes = keep.tile([P, TOKEN_TILES, COL_TILES, P], I32, align_bytes=64)
        red_scales = keep.tile([P, TOKEN_TILES, COL_TILES, P], U8, align_bytes=64)
        red_bf16 = keep.tile([P, TOKEN_TILES, COL_TILES, PACK, P], BF16)
        red_grouped = keep.tile([P, TOKEN_TILES, COL_TILES * P * PACK], BF16, align_bytes=64)
        for h in range(TOKEN_TILES):
            for c in range(COL_TILES):
                copy_on(nc, c, out=red_bf16[:, h, c], in_=reduced[h][c][:].rearrange("p (q t) -> p t q", t=PACK))
        for h in range(TOKEN_TILES):
            for c in range(COL_TILES):
                rt = psum_t.tile([P, PACK, P], BF16, tag="transposed")
                for t in range(PACK):
                    nc.tensor.transpose(rt[:, t, :], red_bf16[:, h, c, t, :], ident_bf16[:])
                copy_on(
                    nc,
                    c,
                    out=red_grouped[:, h, c * P * PACK : (c + 1) * P * PACK].rearrange("p (i t) -> p i t", t=PACK),
                    in_=rt[:].rearrange("p t i -> p i t"),
                )
            for c in range(COL_TILES):
                nc.vector.quantize_mx(
                    out=red_codes[:, h, c, :].bitcast(FP8X4),
                    scales=red_scales[:, h, c, :],
                    in_=red_grouped[:, h, c * P * PACK : (c + 1) * P * PACK],
                )

        result = keep.tile([P, TOKEN_TILES, WIDTH], F32)
        for c in range(COL_TILES):
            cols = slice(c * N_TILE, (c + 1) * N_TILE)
            for h in range(TOKEN_TILES):
                total = psum_acc.tile([P, N_TILE], F32, tag="acc")
                for g in range(PASSES):
                    kh = g // RANKS
                    weight_pass(nc, total, red_codes[:, h, kh, :], red_scales[:, h, kh, :], w2_words, w2_planes, g, c)
                copy_on(nc, h, out=result[:, h, cols], in_=total[:])
                nc.sync.dma_start(
                    out=out.rearrange("r (p h) n -> p r h n", h=TOKEN_TILES)[:, :, h, cols],
                    in_=result[:, h, cols].unsqueeze(1).to_broadcast([P, RANKS, N_TILE]),
                )
